import numpy as np
import ml_dtypes


def mxq(x, axis, fmt="e4m3"):
    dtype, down = {"e4m3": (ml_dtypes.float8_e4m3fn, 7), "e5m2": (ml_dtypes.float8_e5m2, 14)}[fmt]
    v = np.moveaxis(np.asarray(x, np.float32).astype(ml_dtypes.bfloat16).astype(np.float64), axis, -1)
    blocks = v.reshape(v.shape[:-1] + (-1, 32))
    amax = np.abs(blocks).max(-1, keepdims=True)
    byte = np.maximum(np.where(amax > 0, np.frexp(amax)[1] - 1 + 127, 0) - down, 1)
    scale = np.exp2(byte - 127.0)
    codes = (blocks / scale).astype(np.float32).astype(dtype).astype(np.float64)
    return np.moveaxis((codes * scale).reshape(v.shape), -1, axis)


WIDE = False


def mx_kscale(k):
    if not WIDE:
        return np.ones(k)
    levels = np.array([10, -10, 5, -5, 0])
    if k % 512:
        return np.exp2(np.random.permutation(np.resize(levels, k // 32))).repeat(32)
    a = np.empty((k // 512, 16))
    for p in range(k // 512):
        a[p, :8] = np.random.permutation(np.resize(levels, 8))
        for g in range(8):
            far = levels[np.abs(levels - a[p, g]) >= 10]
            a[p, g + 8] = far[np.random.randint(len(far))]
    return np.exp2(a.ravel()).repeat(32)


BF16 = ml_dtypes.bfloat16


def bf(x):
    return np.asarray(x, np.float32).astype(BF16)


def f64(x):
    return np.asarray(x).astype(np.float64)


N, C, F, G = 2048, 3, 512, 256
F2 = F + F
EPS = 1e-08


def silu(v):
    return v / (1.0 + np.exp(-v))


def setup_inputs():
    s, u = mx_kscale(F), mx_kscale(F)
    w1 = np.random.standard_normal((G, F2)) / np.sqrt(F2)
    w1[:, :F] = w1[:, :F] / u
    return {"q": bf(np.random.standard_normal((N, 1, F)) * u),
            "mu": bf(np.random.standard_normal((N, C, F)) * s),
            "W_mix": bf(np.random.standard_normal((F2, F)) / np.sqrt(F) / s),
            "W1": bf(w1),
            "b1": bf(0.2 * np.random.standard_normal(G))}


def reference(q, mu, W_mix, W1, b1):
    mu_mix = mxq(f64(mu), 2, "e4m3") @ mxq(f64(W_mix), 1, "e4m3").T
    mu_V, mu_W = mu_mix[..., :F], mu_mix[..., F:]
    mu_Vn = np.sqrt(np.sum(mu_V * mu_V, axis=1, keepdims=True) + EPS)
    ctx = np.concatenate([f64(q), mu_Vn], axis=-1)
    h = silu((mxq(ctx, 2, "e4m3") @ mxq(f64(W1), 1, "e4m3").T) + f64(b1))
    mu_VW = np.sum(mu_V * mu_W, axis=1, keepdims=True)
    return h, mu_W, mu_VW

@@ -1,0 +1,470 @@
+from contextlib import ExitStack
+
+import concourse.mybir as mybir
+from concourse.masks import make_identity
+
+F32 = mybir.dt.float32
+BF16 = mybir.dt.bfloat16
+U32 = mybir.dt.uint32
+U8 = mybir.dt.uint8
+FP8X4 = mybir.dt.float8_e4m3fn_x4
+ACT = mybir.ActivationFunctionType
+ALU = mybir.AluOpType
+
+P = 128
+N_ATOMS, C, F, G = 2048, 3, 512, 256
+NT = N_ATOMS // P
+EPS = 1e-08
+FLOPS = 2 * N_ATOMS * C * (2 * F) * F + 2 * N_ATOMS * G * (2 * F)
+
+MU_CHUNKS = [(0, 1), (1, 2), (2, 4), (4, 8), (8, 12), (12, 16)]
+Q_CHUNKS = [(0, 2), (2, 4), (4, 8), (8, 16)]
+SILU_CHUNKS = [(0, 4), (4, 8), (8, 12), (12, 14), (14, 16)]
+
+BANKS = {"dmy": ("w", 2), "vs": ("misc", 2), "w": ("w", 2), "v": ("v", 3), "tin": ("misc", 2), "h": ("misc", 2), "ss": ("ss", 1), "wm": ("v", 3), "w1": ("misc", 2)}
+
+PE_PAT = [("mixw", 0, 0), ("mixv", 0, 0), ("mixw", 0, 1), ("mixv", 0, 1), ("mixw", 0, 2), ("mixv", 0, 2), ("mxh", -2, 0),
+          ("tin", 2, 0), ("tacc", -1, 0), ("tacc", -1, 1), ("tacc", -1, 2), ("tin", 2, 1)]
+S_PAT = [("cw", 0, 0), ("sq", 0, 0), ("cw", 0, 1), ("sq", 0, 1), ("cw", 0, 2), ("sq", 0, 2), ("srt", -1, 0)]
+V_PAT = [("cpo", 1, 1), ("qvn", -2, 0), ("quant", 1, 0), ("pr", 0, 0), ("bia", -2, 0), ("cpo", 2, 0), ("pr", 0, 1), ("pr", 0, 2)]
+G_PAT = [("add", 0, 1), ("add", 0, 2)]
+SP_PAT = [("stw", 0, 0), ("stvw", -1, 0)]
+IT_LO, IT_HI = -3, NT + 4
+HEAD = {
+    "pe": [("wmt", 0, 0), ("wmt", 0, 1), ("tin", 0, 0), ("tin", 0, 1), ("wmt", 1, 0), ("wmt", 1, 1)],
+    "s": [("wmc", 0, 1), ("cpo", 0, 1), ("wmc", 1, 1)],
+    "v": [("wmc", 0, 0), ("cpo", 0, 0), ("qwm", 0, 0), ("quant", 0, 0), ("wmc", 1, 0), ("qwm", 1, 0)],
+}
+SPLICE = {
+    "pe": [(("tin", 3, 0), [("w1t", 0, 0)]), (("tin", 4, 0), [("w1t", 1, 0)]), (("tin", 5, 0), [("b1m", 0, 0)])],
+    "v": [(("cpo", 3, 0), [("w1c", 0, 0)]), (("cpo", 4, 0), [("w1c", 1, 0)]), (("cpo", 5, 0), [("b1c", 0, 0)]), (("qvn", 0, 0), [("qw1", 0, 0)])],
+}
+BANK_OVERRIDE = {}
+TAIL = {}
+LATE = ()
+S_CPO = ((0, 1),)
+V_CW = ()
+LATE_LOADS = {1: [("mu", 4), ("q", 3)], 4: [("mu", 5)]}
+
+PE_PAT = [('tin', 2, 0), ('tacc', -1, 0), ('tacc', -1, 1), ('tacc', -1, 2), ('tin', 2, 1), ('mixw', 0, 2),
+ ('mixv', 0, 2), ('mxh', -3, 0), ('mixv', 1, 0), ('mixw', 1, 0), ('mixw', 1, 1), ('mixv', 1, 1)]
+S_PAT = [('sq', 0, 0), ('cw', 0, 0), ('cw', 0, 1), ('sq', 0, 1), ('srt', -1, 0), ('cw', 0, 2), ('sq', 0, 2)]
+V_PAT = [('cw', -1, 2), ('pr', -1, 2), ('cw', 0, 1), ('cpo', 2, 0), ('cw', 0, 0), ('pr', 0, 0), ('cpo', 2, 1),
+ ('pr', 0, 1), ('quant', 2, 0), ('qvn', -2, 0), ('bia', -3, 0)]
+G_PAT = [('add', 0, 1), ('add', -1, 2)]
+V_CW = ((14, 1), (14, 2), (15, 1), (15, 2))
+HEAD = {'pe': [('dmy', 0, 0), ('dmy', 1, 0), ('dmy', 2, 0), ('dmy', 3, 0), ('dmy', 4, 0), ('dmy', 5, 0),
+        ('dmy', 6, 0), ('dmy', 8, 0), ('dmy', 7, 0), ('wmt', 0, 0), ('wmt', 0, 1), ('tin', 0, 0),
+        ('tin', 0, 1), ('dmy', 10, 0), ('dmy', 9, 0), ('wmt', 1, 0), ('wmt', 1, 1), ('tin', 1, 0),
+        ('mixv', 0, 0), ('mixv', 0, 1), ('mixv', 0, 2), ('tin', 1, 1), ('mixw', 0, 0), ('mixw', 0, 1)],
+ 's': [('wmc', 0, 1), ('cpo', 0, 1), ('wmc', 1, 1), ('sq', 0, 0), ('sq', 0, 1), ('sq', 0, 2), ('cw', 0, 0),
+       ('cw', 0, 1), ('cw', 0, 2)],
+ 'v': [('wmc', 0, 0), ('cpo', 0, 0), ('qwm', 0, 0), ('quant', 0, 0), ('wmc', 1, 0), ('qwm', 1, 0),
+       ('cpo', 1, 0), ('cpo', 1, 1), ('quant', 1, 0)]}
+SP_PAT = [('stw', 0, 0), ('stvw', -1, 0)]
+TAIL = {'g': [('add', 13, 2), ('add', 15, 1), ('add', 14, 2), ('add', 15, 2)],
+ 'pe': [('mixv', 14, 0), ('mixw', 14, 0), ('mixw', 14, 1), ('mixv', 14, 1), ('tacc', 13, 0), ('tacc', 13, 1),
+        ('tacc', 13, 2), ('mixw', 14, 2), ('mixv', 14, 2), ('mxh', 11, 0), ('mixv', 15, 0), ('mixw', 15, 0),
+        ('mixw', 15, 1), ('mixv', 15, 1), ('tacc', 14, 0), ('tacc', 14, 1), ('tacc', 14, 2), ('mixw', 15, 2),
+        ('mixv', 15, 2), ('mxh', 12, 0), ('tacc', 15, 0), ('tacc', 15, 1), ('tacc', 15, 2), ('mxh', 13, 0),
+        ('mxh', 14, 0), ('mxh', 15, 0)],
+ 's': [('cw', 14, 0), ('sq', 14, 0), ('sq', 14, 1), ('srt', 13, 0), ('sq', 14, 2), ('sq', 15, 0),
+       ('cw', 15, 0), ('sq', 15, 1), ('srt', 14, 0), ('sq', 15, 2), ('srt', 15, 0), ('silu', 0, 4),
+       ('silu', 4, 8), ('silu', 8, 12), ('silu', 12, 14), ('silu', 14, 16)],
+ 'sp': [('stw', 13, 0), ('stvw', 12, 0), ('stw', 14, 0), ('stvw', 13, 0), ('stw', 15, 0), ('stvw', 14, 0),
+        ('stvw', 15, 0), ('sth', 0, 4), ('sth', 4, 8), ('sth', 8, 12), ('sth', 12, 14), ('sth', 14, 16)],
+ 'v': [('pr', 13, 2), ('cw', 14, 1), ('pr', 14, 0), ('cw', 14, 2), ('pr', 14, 1), ('qvn', 12, 0),
+       ('bia', 11, 0), ('pr', 14, 2), ('cw', 15, 1), ('pr', 15, 0), ('pr', 15, 1), ('qvn', 13, 0),
+       ('bia', 12, 0), ('cw', 15, 2), ('pr', 15, 2), ('bia', 13, 0), ('qvn', 14, 0), ('qvn', 15, 0),
+       ('bia', 14, 0), ('bia', 15, 0)]}
+
+
+def tile_painnmixing_pa_t_kernel(tc, q, mu, W_mix, W1, b1, out_0, out_1, out_2):
+    nc = tc.nc
+    with ExitStack() as ctx:
+        const = ctx.enter_context(tc.tile_pool(name="const", bufs=1))
+        work = ctx.enter_context(tc.tile_pool(name="work", bufs=2))
+        psum = ctx.enter_context(tc.psum_pool(name="psum", bufs=1))
+        ctx.enter_context(tc.manual_schedule())
+
+        q_v = q.rearrange("(p t) o k -> p t (o k)", t=NT)
+        mu_v = mu.rearrange("(p t) c k -> p t c k", t=NT)
+        h_v = out_0.rearrange("(p t) o g -> p t (o g)", t=NT)
+        muw_v = out_1.rearrange("(p t) c f -> p t (c f)", t=NT)
+        vw_v = out_2.rearrange("(p t) o f -> p t (o f)", t=NT)
+        wm_v = [W_mix[0:F, :].rearrange("(p r) k -> p r k", r=4), W_mix[F:2 * F, :].rearrange("(r p) k -> p r k", p=P)]
+        w1_v = W1.rearrange("(r p) k -> p r k", p=P)
+
+        mu_sb = [const.tile([P, t1 - t0, C, F], BF16, name="mu_sb%d" % j) for j, (t0, t1) in enumerate(MU_CHUNKS)]
+        q_sb = [const.tile([P, t1 - t0, F], BF16, name="q_sb%d" % j) for j, (t0, t1) in enumerate(Q_CHUNKS)]
+        wm_sb = [const.tile([P, 4, F], BF16, name="wm_sb%d" % j) for j in range(2)]
+        w1_sb = const.tile([P, 2, 2 * F], BF16, name="w1_sb")
+        b1_row = const.tile([P, G], BF16, name="b1_row")
+        ones_b = const.tile([P, P], BF16, name="ones_b")
+        zer_b = const.tile([P, F], BF16, name="zer_b")
+        b1_f = const.tile([P, G], F32, name="b1_f")
+        ident_f = const.tile([P, P], F32, name="ident_f")
+        eps_t = const.tile([P, 1], F32, name="eps_t")
+        warm = const.tile([P, 1], F32, name="warm")
+        wm_g = [const.tile([P, 4, P, 4], BF16, name="wm_g%d" % j, align_bytes=64) for j in range(2)]
+        wm_codes = const.tile([P, 2 * F], U32, name="wm_codes", align_bytes=64)
+        wm_scales = const.tile([P, 2 * F], U8, name="wm_scales", align_bytes=64)
+        w1_g = const.tile([P, 2, 2, P, 4], BF16, name="w1_g", align_bytes=64)
+        w1_codes = const.tile([P, 2, G], U32, name="w1_codes", align_bytes=64)
+        w1_scales = const.tile([P, 2, G], U8, name="w1_scales", align_bytes=64)
+        hpre = const.tile([P, NT, G], F32, name="hpre")
+
+        turn = {}
+
+        def bank(kind, shape, dtype, i=-1):
+            group, bufs = BANK_OVERRIDE.get((kind, i), BANKS[kind])
+            k = turn.get(group, 0)
+            turn[group] = k + 1
+            return psum.tile(shape, dtype, name=kind + "_ps", tag="%s%d" % (group, k % bufs), bufs=1)
+
+        def mu_rows(i, c):
+            for j, (t0, t1) in enumerate(MU_CHUNKS):
+                if t0 <= i < t1:
+                    return mu_sb[j][:].bitcast(F32)[:, i - t0, c, :]
+            return None
+
+        def q_rows(i):
+            for j, (t0, t1) in enumerate(Q_CHUNKS):
+                if t0 <= i < t1:
+                    return q_sb[j][:].bitcast(F32)[:, i - t0, :]
+            return None
+
+        def load_mu(j):
+            t0, t1 = MU_CHUNKS[j]
+            nc.sync.dma_start(out=mu_sb[j][:], in_=mu_v[:, t0:t1, :, :])
+
+        def load_q(j):
+            t0, t1 = Q_CHUNKS[j]
+            nc.sync.dma_start(out=q_sb[j][:], in_=q_v[:, t0:t1, :])
+
+        nc.vector.memset(b1_row[:], 0.0)
+        nc.vector.memset(ones_b[:], 1.0)
+        nc.vector.memset(zer_b[:], 0.0)
+        nc.sync.dma_start(out=wm_sb[0][:], in_=wm_v[0])
+        load_mu(0)
+        load_q(0)
+        nc.sync.dma_start(out=wm_sb[1][:], in_=wm_v[1])
+        load_mu(1)
+        load_mu(2)
+        load_q(1)
+        nc.sync.dma_start(out=w1_sb[:], in_=w1_v)
+        nc.sync.dma_start(out=b1_row[0:1, :], in_=b1.rearrange("(o g) -> o g", o=1))
+        load_mu(3)
+        load_q(2)
+
+        nc.vector.memset(eps_t[:], EPS)
+        make_identity(nc, ident_f[:])
+        nc.scalar.activation(out=warm[:], in_=eps_t[:], func=ACT.Sqrt)
+
+        st = {}
+
+        def word_transposes(dst, sources):
+            for r, src in enumerate(sources):
+                for u in range(2):
+                    nc.tensor.transpose(dst[:, r, u, :], src[:, u:2 * P:2], ident_f[:])
+
+        def copy_out(eng, dst, src):
+            if eng == "v":
+                nc.vector.tensor_copy(out=dst, in_=src)
+            else:
+                nc.scalar.copy(out=dst, in_=src)
+
+        def op_tin(eng, i, half):
+            dst = bank("tin", [P, 2, 2, P], F32)
+            if ("g", i) not in st:
+                st["g", i] = work.tile([P, 4, P, 4], BF16, name="g", tag="g", bufs=3, align_bytes=64)
+            if half == 0:
+                word_transposes(dst, [mu_rows(i, 0), mu_rows(i, 1)])
+            else:
+                word_transposes(dst, [mu_rows(i, 2), q_rows(i)])
+            st["tin", i, half] = dst
+
+        def op_cpo(eng, i, half):
+            copy_out(eng, st["g", i][:].bitcast(F32)[:, 2 * half:2 * half + 2, :, :],
+                     st["tin", i, half][:].rearrange("p r u a -> p r a u"))
+
+        def op_quant(eng, i, a):
+            codes = work.tile([P, 4 * P], U32, name="codes", tag="codes", bufs=6, align_bytes=64)
+            scales = work.tile([P, 4 * P], U8, name="scales", tag="scales", bufs=6, align_bytes=64)
+            nc.vector.quantize_mx(out=codes[:].bitcast(FP8X4), scales=scales[:],
+                                  in_=st["g", i][:].rearrange("p r a t -> p (r a t)"))
+            st["codes", i] = codes
+            st["scales", i] = scales
+
+        def mix_one(i, c, which):
+            codes, scales = st["codes", i], st["scales", i]
+            dst = bank(which, [P, F], F32, i)
+            lo = F if which == "w" else 0
+            nc.tensor.matmul_mx(
+                out=dst[:],
+                lhsT=codes[:, c * P:(c + 1) * P].bitcast(FP8X4),
+                lhsT_scale=scales[:, c * P:(c + 1) * P],
+                rhs=wm_codes[:, lo:lo + F].bitcast(FP8X4),
+                rhs_scale=wm_scales[:, lo:lo + F],
+                start=True,
+                stop=True,
+            )
+            st[which, i, c] = dst
+
+        def op_mixw(eng, i, c):
+            mix_one(i, c, "w")
+
+        def op_mixv(eng, i, c):
+            mix_one(i, c, "v")
+
+        def op_mixs(eng, i, c):
+            mix_one(i, c, "vs")
+
+        def op_cw(eng, i, c):
+            if ("wout", i) not in st:
+                st["wout", i] = work.tile([P, C, F], F32, name="wout", tag="wout", bufs=4)
+            copy_out(eng, st["wout", i][:, c, :], st["w", i, c][:])
+
+        def op_sq(eng, i, c):
+            sq_t = work.tile([P, F], F32, name="sq", tag="sq", bufs=8)
+            nc.scalar.activation(out=sq_t[:], in_=st["vs" if i in LATE else "v", i, c][:], func=ACT.Square)
+            st["sq", i, c] = sq_t
+
+        def op_pr(eng, i, c):
+            prod = work.tile([P, F], F32, name="prod", tag="prod", bufs=6)
+            nc.vector.tensor_tensor(out=prod[:].rearrange("p (m t) -> p m t", t=4),
+                                    in0=st["v", i, c][:].rearrange("p (t m) -> p m t", t=4),
+                                    in1=st["wout", i][:, c, :].rearrange("p (m t) -> p m t", t=4), op=ALU.mult)
+            st["prod", i, c] = prod
+
+        def op_add(eng, i, c):
+            if c == 1:
+                acc = work.tile([P, F], F32, name="acc", tag="acc", bufs=2)
+                nc.gpsimd.tensor_tensor(out=acc[:], in0=st["prod", i, 0][:], in1=st["prod", i, 1][:], op=ALU.add)
+                st["acc", i] = acc
+            else:
+                vw = work.tile([P, F], F32, name="vw", tag="vw", bufs=4)
+                nc.gpsimd.tensor_tensor(out=vw[:], in0=st["acc", i][:], in1=st["prod", i, 2][:], op=ALU.add)
+                st["vw", i] = vw
+
+        def op_tacc(eng, i, c):
+            if c == 0:
+                st["ss", i] = bank("ss", [P, 4, P], F32, i)
+            ss = st["ss", i]
+            for t in range(4):
+                nc.tensor.matmul(out=ss[:, t, :], lhsT=st["sq", i, c][:, t * P:(t + 1) * P], rhs=ident_f[:],
+                                 is_transpose=True, start=(c == 0 and t == 0), stop=(c == C - 1 and t == 3))
+
+        def op_srt(eng, i, a):
+            vn_g = work.tile([P, P, 4], BF16, name="vn_g", tag="vn_g", bufs=3, align_bytes=64)
+            nc.scalar.activation(out=vn_g[:], in_=st["ss", i][:].rearrange("p t a -> p a t"), func=ACT.Sqrt,
+                                 bias=eps_t[:, 0:1], scale=1.0)
+            st["vn_g", i] = vn_g
+
+        def op_qvn(eng, i, a):
+            vn_codes = work.tile([P, P], U32, name="vn_codes", tag="vn_codes", bufs=3, align_bytes=64)
+            vn_scales = work.tile([P, P], U8, name="vn_scales", tag="vn_scales", bufs=3, align_bytes=64)
+            nc.vector.quantize_mx(out=vn_codes[:].bitcast(FP8X4), scales=vn_scales[:],
+                                  in_=st["vn_g", i][:].rearrange("p a t -> p (a t)"))
+            st["vn_codes", i] = vn_codes
+            st["vn_scales", i] = vn_scales
+
+        def op_mxh(eng, i, a):
+            h_ps = bank("h", [P, G], F32, i)
+            nc.tensor.matmul_mx(out=h_ps[:], lhsT=st["codes", i][:, 3 * P:4 * P].bitcast(FP8X4),
+                                lhsT_scale=st["scales", i][:, 3 * P:4 * P], rhs=w1_codes[:, 0, :].bitcast(FP8X4),
+                                rhs_scale=w1_scales[:, 0, :], start=True, stop=False)
+            nc.tensor.matmul_mx(out=h_ps[:], lhsT=st["vn_codes", i][:].bitcast(FP8X4), lhsT_scale=st["vn_scales", i][:],
+                                rhs=w1_codes[:, 1, :].bitcast(FP8X4), rhs_scale=w1_scales[:, 1, :], start=False, stop=True)
+            st["h_ps", i] = h_ps
+
+        def op_bia(eng, i, a):
+            nc.vector.tensor_tensor(out=hpre[:, i, :], in0=st["h_ps", i][:], in1=b1_f[:], op=ALU.add)
+
+        def op_wmt(eng, j, b):
+            wf = wm_sb[j][:].bitcast(F32)
+            dst = bank("wm", [P, 2, 2, P], F32)
+            word_transposes(dst, [wf[:, 2 * b, :], wf[:, 2 * b + 1, :]])
+            st["wm_ps", j, b] = dst
+
+        def op_wmc(eng, j, b):
+            copy_out(eng, wm_g[j][:].bitcast(F32)[:, 2 * b:2 * b + 2, :, :],
+                     st["wm_ps", j, b][:].rearrange("p r u a -> p r a u"))
+
+        def op_qwm(eng, j, a):
+            nc.vector.quantize_mx(out=wm_codes[:, j * F:(j + 1) * F].bitcast(FP8X4),
+                                  scales=wm_scales[:, j * F:(j + 1) * F],
+                                  in_=wm_g[j][:].rearrange("p r a t -> p (r a t)"))
+
+        def op_w1t(eng, j, a):
+            wf = w1_sb[:].bitcast(F32)
+            dst = bank("w1", [P, 2, 2, P], F32)
+            word_transposes(dst, [wf[:, 0, j * 2 * P:(j + 1) * 2 * P], wf[:, 1, j * 2 * P:(j + 1) * 2 * P]])
+            st["w1_ps", j] = dst
+
+        def op_w1c(eng, j, a):
+            copy_out(eng, w1_g[:].bitcast(F32)[:, j, :, :, :], st["w1_ps", j][:].rearrange("p r u a -> p r a u"))
+
+        def op_b1m(eng, j, a):
+            dst = bank("w1", [P, G], F32)
+            nc.tensor.matmul(out=dst[:], lhsT=ones_b[:], rhs=b1_row[:], start=True, stop=True)
+            st["b1_ps"] = dst
+
+        def op_dmy(eng, j, a):
+            dst = bank("dmy", [P, F], F32)
+            nc.tensor.matmul(out=dst[:], lhsT=ones_b[:], rhs=zer_b[:], start=True, stop=True)
+
+        def op_b1c(eng, j, a):
+            nc.vector.tensor_copy(out=b1_f[:], in_=st["b1_ps"][:])
+
+        def op_qw1(eng, j, a):
+            nc.vector.quantize_mx(out=w1_codes[:].rearrange("p j g -> p (j g)").bitcast(FP8X4),
+                                  scales=w1_scales[:].rearrange("p j g -> p (j g)"),
+                                  in_=w1_g[:].rearrange("p j r a t -> p (j r a t)"))
+
+        def op_stw(eng, i, a):
+            nc.sync.dma_start(out=muw_v[:, i, :], in_=st["wout", i][:].rearrange("p c f -> p (c f)"))
+            for kind, j in LATE_LOADS.get(i, []):
+                if kind == "mu":
+                    load_mu(j)
+                else:
+                    load_q(j)
+
+        def op_stvw(eng, i, a):
+            nc.sync.dma_start(out=vw_v[:, i, :], in_=st["vw", i][:])
+
+        def op_silu(eng, t0, t1):
+            nc.scalar.activation(out=hpre[:, t0:t1, :], in_=hpre[:, t0:t1, :], func=ACT.Silu)
+
+        def op_sth(eng, t0, t1):
+            nc.sync.dma_start(out=h_v[:, t0:t1, :], in_=hpre[:, t0:t1, :])
+
+        OPS = {"tin": op_tin, "cpo": op_cpo, "quant": op_quant, "mixw": op_mixw, "mixv": op_mixv, "mixs": op_mixs, "cw": op_cw,
+               "sq": op_sq, "pr": op_pr, "add": op_add, "tacc": op_tacc, "srt": op_srt, "qvn": op_qvn, "mxh": op_mxh,
+               "bia": op_bia, "wmt": op_wmt, "wmc": op_wmc, "qwm": op_qwm, "w1t": op_w1t, "w1c": op_w1c, "qw1": op_qw1, "b1m": op_b1m, "b1c": op_b1c, "dmy": op_dmy,
+               "stw": op_stw, "stvw": op_stvw, "silu": op_silu, "sth": op_sth}
+
+        def needs(op):
+            n, i, a = op
+            if n == "cpo":
+                return [("tin", i, a)]
+            if n == "quant":
+                return [("cpo", i, 0), ("cpo", i, 1)]
+            if n == "mixw":
+                return [("quant", i, 0), ("qwm", 1, 0)]
+            if n == "mixv" or n == "mixs":
+                return [("quant", i, 0), ("qwm", 0, 0)]
+            if n == "cw":
+                return [("mixw", i, a)]
+            if n == "sq":
+                return [("mixs" if i in LATE else "mixv", i, a)]
+            if n == "pr":
+                return [("cw", i, a), ("mixv", i, a)] + ([] if i in LATE else [("sq", i, a)])
+            if n == "add":
+                return [("pr", i, 0), ("pr", i, 1)] if a == 1 else [("add", i, 1), ("pr", i, 2)]
+            if n == "tacc":
+                return [("sq", i, a)] + ([("tacc", i, a - 1)] if a > 0 else [])
+            if n == "srt":
+                return [("tacc", i, 2)]
+            if n == "qvn":
+                return [("srt", i, 0)]
+            if n == "mxh":
+                return [("qvn", i, 0), ("qw1", 0, 0)]
+            if n == "bia":
+                return [("mxh", i, 0), ("b1c", 0, 0)]
+            if n == "b1c":
+                return [("b1m", 0, 0)]
+            if n == "wmc":
+                return [("wmt", i, a)]
+            if n == "qwm":
+                return [("wmc", i, 0), ("wmc", i, 1)]
+            if n == "w1c":
+                return [("w1t", i, 0)]
+            if n == "qw1":
+                return [("w1c", 0, 0), ("w1c", 1, 0)]
+            if n == "stw":
+                return [("cw", i, 0), ("cw", i, 1), ("cw", i, 2)]
+            if n == "stvw":
+                return [("add", i, 2)]
+            if n == "silu":
+                return [("bia", t, 0) for t in range(i, a)] + [("srt", NT - 1, 0)]
+            if n == "sth":
+                return [("silu", i, a)]
+            return []
+
+        def users(op):
+            n, i, a = op
+            if n == "tin":
+                return [("cpo", i, a)]
+            if n == "mixw":
+                return [("cw", i, a)]
+            if n == "mixv":
+                return [("pr", i, a)] + ([] if i in LATE else [("sq", i, a)])
+            if n == "mixs":
+                return [("sq", i, a)]
+            if n == "tacc":
+                return [("srt", i, 0)]
+            if n == "mxh":
+                return [("bia", i, 0)]
+            if n == "wmt":
+                return [("wmc", i, a)]
+            if n == "w1t":
+                return [("w1c", i, 0)]
+            if n == "b1m":
+                return [("b1c", 0, 0)]
+            return []
+
+        KIND = {"b1m": "w1", "dmy": "dmy", "tin": "tin", "mixw": "w", "mixv": "v", "mixs": "vs", "tacc": "ss", "mxh": "h", "wmt": "wm", "w1t": "w1"}
+
+        pats = {"pe": PE_PAT, "s": S_PAT, "v": V_PAT, "g": G_PAT, "sp": SP_PAT}
+        lists = {}
+        for eng in ("pe", "s", "v", "g", "sp"):
+            seq = list(HEAD.get(eng, []))
+            done = set(seq)
+            for other in TAIL:
+                for op in TAIL[other]:
+                    done.add(op)
+            for it in range(IT_LO, IT_HI):
+                for n, off, a in pats[eng]:
+                    op = (n, it + off, a)
+                    if not 0 <= it + off < NT or op in done:
+                        continue
+                    if n == "cpo" and ((op[1], a) in S_CPO) != (eng == "s"):
+                        continue
+                    if n == "cw" and ((op[1], a) in V_CW) != (eng == "v"):
+                        continue
+                    if n == "mixs":
+                        continue
+                    seq.append(op)
+                    done.add(op)
+            for before, extra in SPLICE.get(eng, []):
+                k = seq.index(before)
+                seq[k:k] = extra
+            lists[eng] = seq + list(TAIL.get(eng, []))
+        if not any(op[0] == "silu" for op in TAIL.get("s", [])):
+            for t0, t1 in SILU_CHUNKS:
+                lists["s"].append(("silu", t0, t1))
+                lists["sp"].append(("sth", t0, t1))
+
+        emitted = set()
+        pos = {eng: 0 for eng in lists}
+        alloc = {}
+        progress = True
+        while progress:
+            progress = False
+            for eng in ("pe", "s", "v", "g", "sp"):
+                while pos[eng] < len(lists[eng]):
+                    op = lists[eng][pos[eng]]
+                    if not all(x in emitted for x in needs(op)):
+                        break
+                    if op[0] in KIND and not (op[0] == "tacc" and op[2] > 0):
+                        tag, bufs = BANK_OVERRIDE.get((KIND[op[0]], op[1]), BANKS[KIND[op[0]]])
+                        hist = alloc.get(tag, [])
+                        if len(hist) >= bufs and not all(x in emitted for x in users(hist[-bufs])):
+                            break
+                        alloc[tag] = hist + [op]
+                    OPS[op[0]](eng, op[1], op[2])
+                    emitted.add(op)
+                    pos[eng] += 1
+                    progress = True
+        assert all(pos[eng] == len(lists[eng]) for eng in lists), "the orders cannot run"

@@ -18,65 +18,33 @@ EPS = 1e-08
 FLOPS = 2 * N_ATOMS * C * (2 * F) * F + 2 * N_ATOMS * G * (2 * F)
 
 MU_CHUNKS = [(0, 1), (1, 2), (2, 4), (4, 8), (8, 12), (12, 16)]
-Q_CHUNKS = [(0, 2), (2, 4), (4, 8), (8, 16)]
+Q_CHUNKS = [(0, 1), (1, 2), (2, 4), (4, 8), (8, 16)]
 SILU_CHUNKS = [(0, 4), (4, 8), (8, 12), (12, 14), (14, 16)]
 
-BANKS = {"dmy": ("w", 2), "vs": ("misc", 2), "w": ("w", 2), "v": ("v", 3), "tin": ("misc", 2), "h": ("misc", 2), "ss": ("ss", 1), "wm": ("v", 3), "w1": ("misc", 2)}
+BANKS = {"dmy": ("w", 2), "w": ("w", 2), "v": ("v", 3), "tin": ("misc", 2), "h": ("misc", 2), "ss": ("ss", 1), "wm": ("v", 3), "w1": ("misc", 2)}
 
-PE_PAT = [("mixw", 0, 0), ("mixv", 0, 0), ("mixw", 0, 1), ("mixv", 0, 1), ("mixw", 0, 2), ("mixv", 0, 2), ("mxh", -2, 0),
-          ("tin", 2, 0), ("tacc", -1, 0), ("tacc", -1, 1), ("tacc", -1, 2), ("tin", 2, 1)]
-S_PAT = [("cw", 0, 0), ("sq", 0, 0), ("cw", 0, 1), ("sq", 0, 1), ("cw", 0, 2), ("sq", 0, 2), ("srt", -1, 0)]
-V_PAT = [("cpo", 1, 1), ("qvn", -2, 0), ("quant", 1, 0), ("pr", 0, 0), ("bia", -2, 0), ("cpo", 2, 0), ("pr", 0, 1), ("pr", 0, 2)]
-G_PAT = [("add", 0, 1), ("add", 0, 2)]
-SP_PAT = [("stw", 0, 0), ("stvw", -1, 0)]
-IT_LO, IT_HI = -3, NT + 4
+PE_STEP = [("tin", 2, 0), ("tacc", -1, 0), ("tacc", -1, 1), ("tacc", -1, 2), ("tin", 2, 1), ("mixw", 0, 2),
+           ("mixv", 0, 2), ("mxh", -3, 0), ("mixv", 1, 0), ("mixw", 1, 0), ("mixw", 1, 1), ("mixv", 1, 1)]
+S_STEP = [("sq", 0, 0), ("cw", 0, 0), ("cw", 0, 1), ("sq", 0, 1), ("srt", -1, 0), ("cw", 0, 2), ("sq", 0, 2)]
+V_STEP = [("pr", -1, 2), ("cpo", 2, 0), ("cw", 0, 1), ("pr", 0, 0), ("cpo", 2, 1), ("cw", 0, 2), ("pr", 0, 1),
+          ("quant", 2, 0), ("qvn", -2, 0), ("bia", -3, 0)]
+G_STEP = [("add", 0, 1), ("add", -1, 2)]
+SP_STEP = [("stw", 0, 0), ("stvw", -1, 0)]
+STEPS = {"pe": PE_STEP, "s": S_STEP, "v": V_STEP, "g": G_STEP, "sp": SP_STEP}
+V_CW = ((14, 1), (14, 2), (15, 1), (15, 2))
 HEAD = {
-    "pe": [("wmt", 0, 0), ("wmt", 0, 1), ("tin", 0, 0), ("tin", 0, 1), ("wmt", 1, 0), ("wmt", 1, 1)],
-    "s": [("wmc", 0, 1), ("cpo", 0, 1), ("wmc", 1, 1)],
-    "v": [("wmc", 0, 0), ("cpo", 0, 0), ("qwm", 0, 0), ("quant", 0, 0), ("wmc", 1, 0), ("qwm", 1, 0)],
+    "pe": [("dmy", k, 0) for k in range(5)] + [
+        ("wmt", 0, 0), ("wmt", 0, 1), ("tin", 0, 0), ("tin", 0, 1), ("wmt", 1, 0), ("wmt", 1, 1), ("tin", 1, 0),
+        ("tin", 1, 1), ("mixv", 0, 0), ("mixv", 0, 1), ("mixw", 0, 0), ("mixw", 0, 1)],
+    "s": [("wmc", 0, 1), ("cpo", 0, 0), ("cpo", 0, 1), ("wmc", 1, 0), ("wmc", 1, 1), ("cpo", 1, 0)],
+    "v": [("wmc", 0, 0), ("qwm", 0, 0), ("quant", 0, 0), ("qwm", 1, 0), ("cpo", 1, 1), ("quant", 1, 0)],
 }
 SPLICE = {
     "pe": [(("tin", 3, 0), [("w1t", 0, 0)]), (("tin", 4, 0), [("w1t", 1, 0)]), (("tin", 5, 0), [("b1m", 0, 0)])],
-    "v": [(("cpo", 3, 0), [("w1c", 0, 0)]), (("cpo", 4, 0), [("w1c", 1, 0)]), (("cpo", 5, 0), [("b1c", 0, 0)]), (("qvn", 0, 0), [("qw1", 0, 0)])],
+    "v": [(("cpo", 3, 0), [("w1c", 0, 0)]), (("cpo", 4, 0), [("w1c", 1, 0)]), (("cpo", 5, 0), [("b1c", 0, 0)]),
+          (("qvn", 0, 0), [("qw1", 0, 0)])],
 }
-BANK_OVERRIDE = {}
-TAIL = {}
-LATE = ()
-S_CPO = ((0, 1),)
-V_CW = ()
-LATE_LOADS = {1: [("mu", 4), ("q", 3)], 4: [("mu", 5)]}
-
-PE_PAT = [('tin', 2, 0), ('tacc', -1, 0), ('tacc', -1, 1), ('tacc', -1, 2), ('tin', 2, 1), ('mixw', 0, 2),
- ('mixv', 0, 2), ('mxh', -3, 0), ('mixv', 1, 0), ('mixw', 1, 0), ('mixw', 1, 1), ('mixv', 1, 1)]
-S_PAT = [('sq', 0, 0), ('cw', 0, 0), ('cw', 0, 1), ('sq', 0, 1), ('srt', -1, 0), ('cw', 0, 2), ('sq', 0, 2)]
-V_PAT = [('cw', -1, 2), ('pr', -1, 2), ('cw', 0, 1), ('cpo', 2, 0), ('cw', 0, 0), ('pr', 0, 0), ('cpo', 2, 1),
- ('pr', 0, 1), ('quant', 2, 0), ('qvn', -2, 0), ('bia', -3, 0)]
-G_PAT = [('add', 0, 1), ('add', -1, 2)]
-V_CW = ((14, 1), (14, 2), (15, 1), (15, 2))
-HEAD = {'pe': [('dmy', 0, 0), ('dmy', 1, 0), ('dmy', 2, 0), ('dmy', 3, 0), ('dmy', 4, 0), ('dmy', 5, 0),
-        ('dmy', 6, 0), ('dmy', 8, 0), ('dmy', 7, 0), ('wmt', 0, 0), ('wmt', 0, 1), ('tin', 0, 0),
-        ('tin', 0, 1), ('dmy', 10, 0), ('dmy', 9, 0), ('wmt', 1, 0), ('wmt', 1, 1), ('tin', 1, 0),
-        ('mixv', 0, 0), ('mixv', 0, 1), ('mixv', 0, 2), ('tin', 1, 1), ('mixw', 0, 0), ('mixw', 0, 1)],
- 's': [('wmc', 0, 1), ('cpo', 0, 1), ('wmc', 1, 1), ('sq', 0, 0), ('sq', 0, 1), ('sq', 0, 2), ('cw', 0, 0),
-       ('cw', 0, 1), ('cw', 0, 2)],
- 'v': [('wmc', 0, 0), ('cpo', 0, 0), ('qwm', 0, 0), ('quant', 0, 0), ('wmc', 1, 0), ('qwm', 1, 0),
-       ('cpo', 1, 0), ('cpo', 1, 1), ('quant', 1, 0)]}
-SP_PAT = [('stw', 0, 0), ('stvw', -1, 0)]
-TAIL = {'g': [('add', 13, 2), ('add', 15, 1), ('add', 14, 2), ('add', 15, 2)],
- 'pe': [('mixv', 14, 0), ('mixw', 14, 0), ('mixw', 14, 1), ('mixv', 14, 1), ('tacc', 13, 0), ('tacc', 13, 1),
-        ('tacc', 13, 2), ('mixw', 14, 2), ('mixv', 14, 2), ('mxh', 11, 0), ('mixv', 15, 0), ('mixw', 15, 0),
-        ('mixw', 15, 1), ('mixv', 15, 1), ('tacc', 14, 0), ('tacc', 14, 1), ('tacc', 14, 2), ('mixw', 15, 2),
-        ('mixv', 15, 2), ('mxh', 12, 0), ('tacc', 15, 0), ('tacc', 15, 1), ('tacc', 15, 2), ('mxh', 13, 0),
-        ('mxh', 14, 0), ('mxh', 15, 0)],
- 's': [('cw', 14, 0), ('sq', 14, 0), ('sq', 14, 1), ('srt', 13, 0), ('sq', 14, 2), ('sq', 15, 0),
-       ('cw', 15, 0), ('sq', 15, 1), ('srt', 14, 0), ('sq', 15, 2), ('srt', 15, 0), ('silu', 0, 4),
-       ('silu', 4, 8), ('silu', 8, 12), ('silu', 12, 14), ('silu', 14, 16)],
- 'sp': [('stw', 13, 0), ('stvw', 12, 0), ('stw', 14, 0), ('stvw', 13, 0), ('stw', 15, 0), ('stvw', 14, 0),
-        ('stvw', 15, 0), ('sth', 0, 4), ('sth', 4, 8), ('sth', 8, 12), ('sth', 12, 14), ('sth', 14, 16)],
- 'v': [('pr', 13, 2), ('cw', 14, 1), ('pr', 14, 0), ('cw', 14, 2), ('pr', 14, 1), ('qvn', 12, 0),
-       ('bia', 11, 0), ('pr', 14, 2), ('cw', 15, 1), ('pr', 15, 0), ('pr', 15, 1), ('qvn', 13, 0),
-       ('bia', 12, 0), ('cw', 15, 2), ('pr', 15, 2), ('bia', 13, 0), ('qvn', 14, 0), ('qvn', 15, 0),
-       ('bia', 14, 0), ('bia', 15, 0)]}
+LATE_LOADS = {1: [("mu", 4), ("q", 4)], 4: [("mu", 5)]}
 
 
 def tile_painnmixing_pa_t_kernel(tc, q, mu, W_mix, W1, b1, out_0, out_1, out_2):
@@ -93,11 +61,12 @@ def tile_painnmixing_pa_t_kernel(tc, q, mu, W_mix, W1, b1, out_0, out_1, out_2):
         muw_v = out_1.rearrange("(p t) c f -> p t (c f)", t=NT)
         vw_v = out_2.rearrange("(p t) o f -> p t (o f)", t=NT)
         wm_v = [W_mix[0:F, :].rearrange("(p r) k -> p r k", r=4), W_mix[F:2 * F, :].rearrange("(r p) k -> p r k", p=P)]
+        wm_half = [[wm_v[j][:, 2 * b:2 * b + 2, :] for b in range(2)] for j in range(2)]
         w1_v = W1.rearrange("(r p) k -> p r k", p=P)
 
         mu_sb = [const.tile([P, t1 - t0, C, F], BF16, name="mu_sb%d" % j) for j, (t0, t1) in enumerate(MU_CHUNKS)]
         q_sb = [const.tile([P, t1 - t0, F], BF16, name="q_sb%d" % j) for j, (t0, t1) in enumerate(Q_CHUNKS)]
-        wm_sb = [const.tile([P, 4, F], BF16, name="wm_sb%d" % j) for j in range(2)]
+        wm_sb = [[const.tile([P, 2, F], BF16, name="wm_sb%d%d" % (j, b)) for b in range(2)] for j in range(2)]
         w1_sb = const.tile([P, 2, 2 * F], BF16, name="w1_sb")
         b1_row = const.tile([P, G], BF16, name="b1_row")
         ones_b = const.tile([P, P], BF16, name="ones_b")
@@ -117,7 +86,7 @@ def tile_painnmixing_pa_t_kernel(tc, q, mu, W_mix, W1, b1, out_0, out_1, out_2):
         turn = {}
 
         def bank(kind, shape, dtype, i=-1):
-            group, bufs = BANK_OVERRIDE.get((kind, i), BANKS[kind])
+            group, bufs = BANKS[kind]
             k = turn.get(group, 0)
             turn[group] = k + 1
             return psum.tile(shape, dtype, name=kind + "_ps", tag="%s%d" % (group, k % bufs), bufs=1)
@@ -145,17 +114,20 @@ def tile_painnmixing_pa_t_kernel(tc, q, mu, W_mix, W1, b1, out_0, out_1, out_2):
         nc.vector.memset(b1_row[:], 0.0)
         nc.vector.memset(ones_b[:], 1.0)
         nc.vector.memset(zer_b[:], 0.0)
-        nc.sync.dma_start(out=wm_sb[0][:], in_=wm_v[0])
+        for b in range(2):
+            nc.sync.dma_start(out=wm_sb[0][b][:], in_=wm_half[0][b])
         load_mu(0)
         load_q(0)
-        nc.sync.dma_start(out=wm_sb[1][:], in_=wm_v[1])
+        for b in range(2):
+            nc.sync.dma_start(out=wm_sb[1][b][:], in_=wm_half[1][b])
         load_mu(1)
-        load_mu(2)
         load_q(1)
+        load_mu(2)
+        load_q(2)
         nc.sync.dma_start(out=w1_sb[:], in_=w1_v)
         nc.sync.dma_start(out=b1_row[0:1, :], in_=b1.rearrange("(o g) -> o g", o=1))
         load_mu(3)
-        load_q(2)
+        load_q(3)
 
         nc.vector.memset(eps_t[:], EPS)
         make_identity(nc, ident_f[:])
@@ -217,9 +189,6 @@ def tile_painnmixing_pa_t_kernel(tc, q, mu, W_mix, W1, b1, out_0, out_1, out_2):
         def op_mixv(eng, i, c):
             mix_one(i, c, "v")
 
-        def op_mixs(eng, i, c):
-            mix_one(i, c, "vs")
-
         def op_cw(eng, i, c):
             if ("wout", i) not in st:
                 st["wout", i] = work.tile([P, C, F], F32, name="wout", tag="wout", bufs=4)
@@ -227,7 +196,7 @@ def tile_painnmixing_pa_t_kernel(tc, q, mu, W_mix, W1, b1, out_0, out_1, out_2):
 
         def op_sq(eng, i, c):
             sq_t = work.tile([P, F], F32, name="sq", tag="sq", bufs=8)
-            nc.scalar.activation(out=sq_t[:], in_=st["vs" if i in LATE else "v", i, c][:], func=ACT.Square)
+            nc.scalar.activation(out=sq_t[:], in_=st["v", i, c][:], func=ACT.Square)
             st["sq", i, c] = sq_t
 
         def op_pr(eng, i, c):
@@ -282,9 +251,9 @@ def tile_painnmixing_pa_t_kernel(tc, q, mu, W_mix, W1, b1, out_0, out_1, out_2):
             nc.vector.tensor_tensor(out=hpre[:, i, :], in0=st["h_ps", i][:], in1=b1_f[:], op=ALU.add)
 
         def op_wmt(eng, j, b):
-            wf = wm_sb[j][:].bitcast(F32)
+            wf = wm_sb[j][b][:].bitcast(F32)
             dst = bank("wm", [P, 2, 2, P], F32)
-            word_transposes(dst, [wf[:, 2 * b, :], wf[:, 2 * b + 1, :]])
+            word_transposes(dst, [wf[:, 0, :], wf[:, 1, :]])
             st["wm_ps", j, b] = dst
 
         def op_wmc(eng, j, b):
@@ -339,7 +308,7 @@ def tile_painnmixing_pa_t_kernel(tc, q, mu, W_mix, W1, b1, out_0, out_1, out_2):
         def op_sth(eng, t0, t1):
             nc.sync.dma_start(out=h_v[:, t0:t1, :], in_=hpre[:, t0:t1, :])
 
-        OPS = {"tin": op_tin, "cpo": op_cpo, "quant": op_quant, "mixw": op_mixw, "mixv": op_mixv, "mixs": op_mixs, "cw": op_cw,
+        OPS = {"tin": op_tin, "cpo": op_cpo, "quant": op_quant, "mixw": op_mixw, "mixv": op_mixv, "cw": op_cw,
                "sq": op_sq, "pr": op_pr, "add": op_add, "tacc": op_tacc, "srt": op_srt, "qvn": op_qvn, "mxh": op_mxh,
                "bia": op_bia, "wmt": op_wmt, "wmc": op_wmc, "qwm": op_qwm, "w1t": op_w1t, "w1c": op_w1c, "qw1": op_qw1, "b1m": op_b1m, "b1c": op_b1c, "dmy": op_dmy,
                "stw": op_stw, "stvw": op_stvw, "silu": op_silu, "sth": op_sth}
@@ -352,14 +321,14 @@ def tile_painnmixing_pa_t_kernel(tc, q, mu, W_mix, W1, b1, out_0, out_1, out_2):
                 return [("cpo", i, 0), ("cpo", i, 1)]
             if n == "mixw":
                 return [("quant", i, 0), ("qwm", 1, 0)]
-            if n == "mixv" or n == "mixs":
+            if n == "mixv":
                 return [("quant", i, 0), ("qwm", 0, 0)]
             if n == "cw":
                 return [("mixw", i, a)]
             if n == "sq":
-                return [("mixs" if i in LATE else "mixv", i, a)]
+                return [("mixv", i, a)]
             if n == "pr":
-                return [("cw", i, a), ("mixv", i, a)] + ([] if i in LATE else [("sq", i, a)])
+                return [("cw", i, a), ("mixv", i, a), ("sq", i, a)]
             if n == "add":
                 return [("pr", i, 0), ("pr", i, 1)] if a == 1 else [("add", i, 1), ("pr", i, 2)]
             if n == "tacc":
@@ -399,9 +368,7 @@ def tile_painnmixing_pa_t_kernel(tc, q, mu, W_mix, W1, b1, out_0, out_1, out_2):
             if n == "mixw":
                 return [("cw", i, a)]
             if n == "mixv":
-                return [("pr", i, a)] + ([] if i in LATE else [("sq", i, a)])
-            if n == "mixs":
-                return [("sq", i, a)]
+                return [("pr", i, a), ("sq", i, a)]
             if n == "tacc":
                 return [("srt", i, 0)]
             if n == "mxh":
@@ -414,37 +381,28 @@ def tile_painnmixing_pa_t_kernel(tc, q, mu, W_mix, W1, b1, out_0, out_1, out_2):
                 return [("b1c", 0, 0)]
             return []
 
-        KIND = {"b1m": "w1", "dmy": "dmy", "tin": "tin", "mixw": "w", "mixv": "v", "mixs": "vs", "tacc": "ss", "mxh": "h", "wmt": "wm", "w1t": "w1"}
+        KIND = {"b1m": "w1", "dmy": "dmy", "tin": "tin", "mixw": "w", "mixv": "v", "tacc": "ss", "mxh": "h", "wmt": "wm", "w1t": "w1"}
 
-        pats = {"pe": PE_PAT, "s": S_PAT, "v": V_PAT, "g": G_PAT, "sp": SP_PAT}
         lists = {}
         for eng in ("pe", "s", "v", "g", "sp"):
             seq = list(HEAD.get(eng, []))
-            done = set(seq)
-            for other in TAIL:
-                for op in TAIL[other]:
-                    done.add(op)
-            for it in range(IT_LO, IT_HI):
-                for n, off, a in pats[eng]:
+            done = set(seq) | {op for e in HEAD for op in HEAD[e] if op[0] == "cpo"}
+            for it in range(-3, NT + 4):
+                for n, off, a in STEPS[eng]:
                     op = (n, it + off, a)
                     if not 0 <= it + off < NT or op in done:
                         continue
-                    if n == "cpo" and ((op[1], a) in S_CPO) != (eng == "s"):
-                        continue
                     if n == "cw" and ((op[1], a) in V_CW) != (eng == "v"):
-                        continue
-                    if n == "mixs":
                         continue
                     seq.append(op)
                     done.add(op)
             for before, extra in SPLICE.get(eng, []):
                 k = seq.index(before)
                 seq[k:k] = extra
-            lists[eng] = seq + list(TAIL.get(eng, []))
-        if not any(op[0] == "silu" for op in TAIL.get("s", [])):
-            for t0, t1 in SILU_CHUNKS:
-                lists["s"].append(("silu", t0, t1))
-                lists["sp"].append(("sth", t0, t1))
+            lists[eng] = seq
+        for t0, t1 in SILU_CHUNKS:
+            lists["s"].append(("silu", t0, t1))
+            lists["sp"].append(("sth", t0, t1))
 
         emitted = set()
         pos = {eng: 0 for eng in lists}
@@ -458,7 +416,7 @@ def tile_painnmixing_pa_t_kernel(tc, q, mu, W_mix, W1, b1, out_0, out_1, out_2):
                     if not all(x in emitted for x in needs(op)):
                         break
                     if op[0] in KIND and not (op[0] == "tacc" and op[2] > 0):
-                        tag, bufs = BANK_OVERRIDE.get((KIND[op[0]], op[1]), BANKS[KIND[op[0]]])
+                        tag, bufs = BANKS[KIND[op[0]]]
                         hist = alloc.get(tag, [])
                         if len(hist) >= bufs and not all(x in emitted for x in users(hist[-bufs])):
                             break

@@ -28,7 +28,7 @@ PE_STEP = [("tin", 2, 0), ("tacc", -1, 0), ("tacc", -1, 1), ("tacc", -1, 2), ("t
 S_STEP = [("sq", 0, 0), ("cw", 0, 0), ("cw", 0, 1), ("sq", 0, 1), ("srt", -1, 0), ("cw", 0, 2), ("sq", 0, 2)]
 V_STEP = [("pr", -1, 2), ("cpo", 2, 0), ("cw", 0, 1), ("pr", 0, 0), ("cpo", 2, 1), ("cw", 0, 2), ("pr", 0, 1),
           ("quant", 2, 0), ("qvn", -2, 0), ("bia", -3, 0)]
-G_STEP = [("add", 0, 1), ("add", -1, 2)]
+G_STEP = [("add", -1, 2), ("add", 0, 1)]
 SP_STEP = [("stw", 0, 0), ("stvw", -1, 0)]
 STEPS = {"pe": PE_STEP, "s": S_STEP, "v": V_STEP, "g": G_STEP, "sp": SP_STEP}
 V_CW = ((14, 1), (14, 2), (15, 1), (15, 2))

@@ -24,10 +24,10 @@ SILU_CHUNKS = [(0, 4), (4, 8), (8, 12), (12, 14), (14, 16)]
 BANKS = {"dmy": ("w", 2), "w": ("w", 2), "v": ("v", 3), "tin": ("misc", 2), "h": ("misc", 2), "ss": ("ss", 1), "wm": ("v", 3), "w1": ("misc", 2)}
 
 PE_STEP = [("tin", 2, 0), ("tacc", -1, 0), ("tacc", -1, 1), ("tacc", -1, 2), ("tin", 2, 1), ("mixw", 0, 2),
-           ("mixv", 0, 2), ("mxh", -3, 0), ("mixv", 1, 0), ("mixw", 1, 0), ("mixw", 1, 1), ("mixv", 1, 1)]
+           ("mixv", 0, 2), ("mxh", -4, 0), ("mixv", 1, 0), ("mixw", 1, 0), ("mixw", 1, 1), ("mixv", 1, 1)]
 S_STEP = [("sq", 0, 0), ("cw", 0, 0), ("cw", 0, 1), ("sq", 0, 1), ("srt", -1, 0), ("cw", 0, 2), ("sq", 0, 2)]
 V_STEP = [("pr", -1, 2), ("cpo", 2, 0), ("cw", 0, 1), ("pr", 0, 0), ("cpo", 2, 1), ("cw", 0, 2), ("pr", 0, 1),
-          ("quant", 2, 0), ("qvn", -2, 0), ("bia", -3, 0)]
+          ("quant", 2, 0), ("qvn", -2, 0), ("bia", -4, 0)]
 G_STEP = [("add", -1, 2), ("add", 0, 1)]
 SP_STEP = [("stw", 0, 0), ("stvw", -1, 0)]
 STEPS = {"pe": PE_STEP, "s": S_STEP, "v": V_STEP, "g": G_STEP, "sp": SP_STEP}
@@ -42,7 +42,7 @@ HEAD = {
 SPLICE = {
     "pe": [(("tin", 3, 0), [("w1t", 0, 0)]), (("tin", 4, 0), [("w1t", 1, 0)]), (("tin", 5, 0), [("b1m", 0, 0)])],
     "v": [(("cpo", 3, 0), [("w1c", 0, 0)]), (("cpo", 4, 0), [("w1c", 1, 0)]), (("cpo", 5, 0), [("b1c", 0, 0)]),
-          (("qvn", 0, 0), [("qw1", 0, 0)])],
+          (("pr", 2, 2), [("qw1", 0, 0)])],
 }
 LATE_LOADS = {1: [("mu", 4), ("q", 4)], 4: [("mu", 5)]}
 
@@ -200,20 +200,21 @@ def tile_painnmixing_pa_t_kernel(tc, q, mu, W_mix, W1, b1, out_0, out_1, out_2):
             st["sq", i, c] = sq_t
 
         def op_pr(eng, i, c):
-            prod = work.tile([P, F], F32, name="prod", tag="prod", bufs=6)
-            nc.vector.tensor_tensor(out=prod[:].rearrange("p (m t) -> p m t", t=4),
+            if c == 0:
+                st["prod", i] = work.tile([P, C, F], F32, name="prod", tag="prod", bufs=3)
+            prod = st["prod", i]
+            nc.vector.tensor_tensor(out=prod[:, c, :].rearrange("p (m t) -> p m t", t=4),
                                     in0=st["v", i, c][:].rearrange("p (t m) -> p m t", t=4),
                                     in1=st["wout", i][:, c, :].rearrange("p (m t) -> p m t", t=4), op=ALU.mult)
-            st["prod", i, c] = prod
 
         def op_add(eng, i, c):
             if c == 1:
                 acc = work.tile([P, F], F32, name="acc", tag="acc", bufs=2)
-                nc.gpsimd.tensor_tensor(out=acc[:], in0=st["prod", i, 0][:], in1=st["prod", i, 1][:], op=ALU.add)
+                nc.gpsimd.tensor_tensor(out=acc[:], in0=st["prod", i][:, 0, :], in1=st["prod", i][:, 1, :], op=ALU.add)
                 st["acc", i] = acc
             else:
                 vw = work.tile([P, F], F32, name="vw", tag="vw", bufs=4)
-                nc.gpsimd.tensor_tensor(out=vw[:], in0=st["acc", i][:], in1=st["prod", i, 2][:], op=ALU.add)
+                nc.gpsimd.tensor_tensor(out=vw[:], in0=st["acc", i][:], in1=st["prod", i][:, 2, :], op=ALU.add)
                 st["vw", i] = vw
 
         def op_tacc(eng, i, c):
@@ -225,25 +226,26 @@ def tile_painnmixing_pa_t_kernel(tc, q, mu, W_mix, W1, b1, out_0, out_1, out_2):
                                  is_transpose=True, start=(c == 0 and t == 0), stop=(c == C - 1 and t == 3))
 
         def op_srt(eng, i, a):
-            vn_g = work.tile([P, P, 4], BF16, name="vn_g", tag="vn_g", bufs=3, align_bytes=64)
-            nc.scalar.activation(out=vn_g[:], in_=st["ss", i][:].rearrange("p t a -> p a t"), func=ACT.Sqrt,
+            if i % 2 == 0:
+                st["vn_g", i // 2] = work.tile([P, 2, P, 4], BF16, name="vn_g", tag="vn_g", bufs=3, align_bytes=64)
+            nc.scalar.activation(out=st["vn_g", i // 2][:, i % 2, :, :], in_=st["ss", i][:].rearrange("p t a -> p a t"), func=ACT.Sqrt,
                                  bias=eps_t[:, 0:1], scale=1.0)
-            st["vn_g", i] = vn_g
 
         def op_qvn(eng, i, a):
-            vn_codes = work.tile([P, P], U32, name="vn_codes", tag="vn_codes", bufs=3, align_bytes=64)
-            vn_scales = work.tile([P, P], U8, name="vn_scales", tag="vn_scales", bufs=3, align_bytes=64)
+            vn_codes = work.tile([P, 2 * P], U32, name="vn_codes", tag="vn_codes", bufs=NT // 2, align_bytes=64)
+            vn_scales = work.tile([P, 2 * P], U8, name="vn_scales", tag="vn_scales", bufs=NT // 2, align_bytes=64)
             nc.vector.quantize_mx(out=vn_codes[:].bitcast(FP8X4), scales=vn_scales[:],
-                                  in_=st["vn_g", i][:].rearrange("p a t -> p (a t)"))
-            st["vn_codes", i] = vn_codes
-            st["vn_scales", i] = vn_scales
+                                  in_=st["vn_g", i // 2][:].rearrange("p j a t -> p (j a t)"))
+            for j in range(2):
+                st["vn_codes", i - 1 + j] = vn_codes[:, j * P:(j + 1) * P]
+                st["vn_scales", i - 1 + j] = vn_scales[:, j * P:(j + 1) * P]
 
         def op_mxh(eng, i, a):
             h_ps = bank("h", [P, G], F32, i)
             nc.tensor.matmul_mx(out=h_ps[:], lhsT=st["codes", i][:, 3 * P:4 * P].bitcast(FP8X4),
                                 lhsT_scale=st["scales", i][:, 3 * P:4 * P], rhs=w1_codes[:, 0, :].bitcast(FP8X4),
                                 rhs_scale=w1_scales[:, 0, :], start=True, stop=False)
-            nc.tensor.matmul_mx(out=h_ps[:], lhsT=st["vn_codes", i][:].bitcast(FP8X4), lhsT_scale=st["vn_scales", i][:],
+            nc.tensor.matmul_mx(out=h_ps[:], lhsT=st["vn_codes", i].bitcast(FP8X4), lhsT_scale=st["vn_scales", i],
                                 rhs=w1_codes[:, 1, :].bitcast(FP8X4), rhs_scale=w1_scales[:, 1, :], start=False, stop=True)
             st["h_ps", i] = h_ps
 
@@ -336,9 +338,9 @@ def tile_painnmixing_pa_t_kernel(tc, q, mu, W_mix, W1, b1, out_0, out_1, out_2):
             if n == "srt":
                 return [("tacc", i, 2)]
             if n == "qvn":
-                return [("srt", i, 0)]
+                return [("srt", i - 1, 0), ("srt", i, 0)]
             if n == "mxh":
-                return [("qvn", i, 0), ("qw1", 0, 0)]
+                return [("qvn", i | 1, 0), ("qw1", 0, 0)]
             if n == "bia":
                 return [("mxh", i, 0), ("b1c", 0, 0)]
             if n == "b1c":
@@ -390,7 +392,7 @@ def tile_painnmixing_pa_t_kernel(tc, q, mu, W_mix, W1, b1, out_0, out_1, out_2):
             for it in range(-3, NT + 4):
                 for n, off, a in STEPS[eng]:
                     op = (n, it + off, a)
-                    if not 0 <= it + off < NT or op in done:
+                    if not 0 <= it + off < NT or op in done or (n == "qvn" and op[1] % 2 == 0):
                         continue
                     if n == "cw" and ((op[1], a) in V_CW) != (eng == "v"):
                         continue

@@ -31,13 +31,22 @@ V_STEP = [("pr", -1, 2), ("cpo", 2, 0), ("cw", 0, 1), ("pr", 0, 0), ("cpo", 2, 1
 G_STEP = [("add", -1, 2), ("add", 0, 1)]
 SP_STEP = [("stw", 0, 0), ("stvw", -1, 0)]
 STEPS = {"pe": PE_STEP, "s": S_STEP, "v": V_STEP, "g": G_STEP, "sp": SP_STEP}
-V_CW = ((14, 1), (14, 2), (15, 1), (15, 2))
+V_CW = ((14, 1), (15, 0), (15, 1))
 HEAD = {
     "pe": [("dmy", k, 0) for k in range(5)] + [
         ("wmt", 0, 0), ("wmt", 0, 1), ("tin", 0, 0), ("tin", 0, 1), ("wmt", 1, 0), ("wmt", 1, 1), ("tin", 1, 0),
         ("tin", 1, 1), ("mixv", 0, 0), ("mixv", 0, 1), ("mixw", 0, 0), ("mixw", 0, 1)],
-    "s": [("wmc", 0, 1), ("cpo", 0, 0), ("cpo", 0, 1), ("wmc", 1, 0), ("wmc", 1, 1), ("cpo", 1, 0)],
-    "v": [("wmc", 0, 0), ("qwm", 0, 0), ("quant", 0, 0), ("qwm", 1, 0), ("cpo", 1, 1), ("quant", 1, 0)],
+    "s": [("wmc", 0, 0), ("cpo", 0, 0), ("wmc", 1, 0), ("wmc", 1, 1), ("cpo", 1, 0), ("cpo", 1, 1)],
+    "v": [("wmc", 0, 1), ("qwm", 0, 0), ("cpo", 0, 1), ("quant", 0, 0), ("qwm", 1, 0), ("quant", 1, 0)],
+}
+TAIL = {
+    "pe": [("mixw", 15, 0), ("mixv", 15, 0), ("mixv", 15, 1), ("tacc", 14, 0), ("tacc", 14, 1), ("tacc", 14, 2),
+           ("mixw", 15, 1), ("mixw", 15, 2), ("mixv", 15, 2), ("mxh", 10, 0), ("tacc", 15, 0), ("tacc", 15, 1),
+           ("tacc", 15, 2)] + [("mxh", i, 0) for i in range(11, 16)],
+    "s": [("cw", 14, 2), ("sq", 14, 2), ("sq", 15, 0), ("sq", 15, 1), ("srt", 14, 0), ("sq", 15, 2), ("cw", 15, 2), ("srt", 15, 0)],
+    "v": [("cw", 14, 1), ("pr", 13, 2), ("pr", 14, 0), ("pr", 14, 1), ("cw", 15, 0), ("pr", 14, 2), ("pr", 15, 0),
+          ("cw", 15, 1), ("pr", 15, 1), ("bia", 9, 0), ("pr", 15, 2), ("qvn", 13, 0), ("bia", 10, 0), ("bia", 11, 0),
+          ("qvn", 15, 0)] + [("bia", i, 0) for i in range(12, 16)],
 }
 SPLICE = {
     "pe": [(("tin", 3, 0), [("w1t", 0, 0)]), (("tin", 4, 0), [("w1t", 1, 0)]), (("tin", 5, 0), [("b1m", 0, 0)])],
@@ -229,7 +238,7 @@ def tile_painnmixing_pa_t_kernel(tc, q, mu, W_mix, W1, b1, out_0, out_1, out_2):
             if i % 2 == 0:
                 st["vn_g", i // 2] = work.tile([P, 2, P, 4], BF16, name="vn_g", tag="vn_g", bufs=3, align_bytes=64)
             nc.scalar.activation(out=st["vn_g", i // 2][:, i % 2, :, :], in_=st["ss", i][:].rearrange("p t a -> p a t"), func=ACT.Sqrt,
-                                 bias=eps_t[:, 0:1], scale=1.0)
+                                 bias=EPS, scale=1.0)
 
         def op_qvn(eng, i, a):
             vn_codes = work.tile([P, 2 * P], U32, name="vn_codes", tag="vn_codes", bufs=NT // 2, align_bytes=64)
@@ -388,7 +397,7 @@ def tile_painnmixing_pa_t_kernel(tc, q, mu, W_mix, W1, b1, out_0, out_1, out_2):
         lists = {}
         for eng in ("pe", "s", "v", "g", "sp"):
             seq = list(HEAD.get(eng, []))
-            done = set(seq) | {op for e in HEAD for op in HEAD[e] if op[0] == "cpo"}
+            done = set(seq) | {op for e in HEAD for op in HEAD[e] if op[0] == "cpo"} | set(TAIL.get(eng, []))
             for it in range(-3, NT + 4):
                 for n, off, a in STEPS[eng]:
                     op = (n, it + off, a)
@@ -398,6 +407,7 @@ def tile_painnmixing_pa_t_kernel(tc, q, mu, W_mix, W1, b1, out_0, out_1, out_2):
                         continue
                     seq.append(op)
                     done.add(op)
+            seq.extend(TAIL.get(eng, []))
             for before, extra in SPLICE.get(eng, []):
                 k = seq.index(before)
                 seq[k:k] = extra

@@ -120,9 +120,9 @@ def tile_painnmixing_pa_t_kernel(tc, q, mu, W_mix, W1, b1, out_0, out_1, out_2):
             t0, t1 = Q_CHUNKS[j]
             nc.sync.dma_start(out=q_sb[j][:], in_=q_v[:, t0:t1, :])
 
+        nc.vector.memset(zer_b[:].bitcast(U32), 0)
         nc.vector.memset(b1_row[:], 0.0)
         nc.vector.memset(ones_b[:], 1.0)
-        nc.vector.memset(zer_b[:], 0.0)
         for b in range(2):
             nc.sync.dma_start(out=wm_sb[0][b][:], in_=wm_half[0][b])
         load_mu(0)
@@ -217,13 +217,14 @@ def tile_painnmixing_pa_t_kernel(tc, q, mu, W_mix, W1, b1, out_0, out_1, out_2):
                                     in1=st["wout", i][:, c, :].rearrange("p (m t) -> p m t", t=4), op=ALU.mult)
 
         def op_add(eng, i, c):
+            prod = st["prod", i]
             if c == 1:
                 acc = work.tile([P, F], F32, name="acc", tag="acc", bufs=2)
-                nc.gpsimd.tensor_tensor(out=acc[:], in0=st["prod", i][:, 0, :], in1=st["prod", i][:, 1, :], op=ALU.add)
+                nc.gpsimd.tensor_tensor(out=acc[:], in0=prod[:, 0, :], in1=prod[:, 1, :], op=ALU.add)
                 st["acc", i] = acc
             else:
                 vw = work.tile([P, F], F32, name="vw", tag="vw", bufs=4)
-                nc.gpsimd.tensor_tensor(out=vw[:], in0=st["acc", i][:], in1=st["prod", i][:, 2, :], op=ALU.add)
+                nc.gpsimd.tensor_tensor(out=vw[:], in0=st["acc", i][:], in1=prod[:, 2, :], op=ALU.add)
                 st["vw", i] = vw
 
         def op_tacc(eng, i, c):
@@ -292,7 +293,7 @@ def tile_painnmixing_pa_t_kernel(tc, q, mu, W_mix, W1, b1, out_0, out_1, out_2):
 
         def op_dmy(eng, j, a):
             dst = bank("dmy", [P, F], F32)
-            nc.tensor.matmul(out=dst[:], lhsT=ones_b[:], rhs=zer_b[:], start=True, stop=True)
+            nc.tensor.matmul(out=dst[:], lhsT=zer_b[:, 0:P], rhs=zer_b[:], start=True, stop=True)
 
         def op_b1c(eng, j, a):
             nc.vector.tensor_copy(out=b1_f[:], in_=st["b1_ps"][:])

from contextlib import ExitStack

import concourse.mybir as mybir
from concourse.masks import make_identity

F32 = mybir.dt.float32
BF16 = mybir.dt.bfloat16
U32 = mybir.dt.uint32
U8 = mybir.dt.uint8
FP8X4 = mybir.dt.float8_e4m3fn_x4
ACT = mybir.ActivationFunctionType
ALU = mybir.AluOpType

P = 128
N_ATOMS, C, F, G = 2048, 3, 512, 256
NT = N_ATOMS // P
EPS = 1e-08
FLOPS = 2 * N_ATOMS * C * (2 * F) * F + 2 * N_ATOMS * G * (2 * F)

MU_CHUNKS = [(0, 1), (1, 2), (2, 4), (4, 8), (8, 12), (12, 16)]
Q_CHUNKS = [(0, 1), (1, 2), (2, 4), (4, 8), (8, 16)]
SILU_CHUNKS = [(0, 4), (4, 8), (8, 12), (12, 14), (14, 16)]

BANKS = {"dmy": ("w", 2), "w": ("w", 2), "v": ("v", 3), "tin": ("misc", 2), "h": ("misc", 2), "ss": ("ss", 1), "wm": ("v", 3), "w1": ("misc", 2)}

PE_STEP = [("tin", 2, 0), ("tacc", -1, 0), ("tacc", -1, 1), ("tacc", -1, 2), ("tin", 2, 1), ("mixw", 0, 2),
           ("mixv", 0, 2), ("mxh", -4, 0), ("mixv", 1, 0), ("mixw", 1, 0), ("mixw", 1, 1), ("mixv", 1, 1)]
S_STEP = [("sq", 0, 0), ("cw", 0, 0), ("cw", 0, 1), ("sq", 0, 1), ("srt", -1, 0), ("cw", 0, 2), ("sq", 0, 2)]
V_STEP = [("pr", -1, 2), ("cpo", 2, 0), ("cw", 0, 1), ("pr", 0, 0), ("cpo", 2, 1), ("cw", 0, 2), ("pr", 0, 1),
          ("quant", 2, 0), ("qvn", -2, 0), ("bia", -4, 0)]
G_STEP = [("add", -1, 2), ("add", 0, 1)]
SP_STEP = [("stw", 0, 0), ("stvw", -1, 0)]
STEPS = {"pe": PE_STEP, "s": S_STEP, "v": V_STEP, "g": G_STEP, "sp": SP_STEP}
V_CW = ((14, 1), (15, 0), (15, 1))
HEAD = {
    "pe": [("dmy", k, 0) for k in range(5)] + [
        ("wmt", 0, 0), ("wmt", 0, 1), ("tin", 0, 0), ("tin", 0, 1), ("wmt", 1, 0), ("wmt", 1, 1), ("tin", 1, 0),
        ("tin", 1, 1), ("mixv", 0, 0), ("mixv", 0, 1), ("mixw", 0, 0), ("mixw", 0, 1)],
    "s": [("wmc", 0, 0), ("cpo", 0, 0), ("wmc", 1, 0), ("wmc", 1, 1), ("cpo", 1, 0), ("cpo", 1, 1)],
    "v": [("wmc", 0, 1), ("qwm", 0, 0), ("cpo", 0, 1), ("quant", 0, 0), ("qwm", 1, 0), ("quant", 1, 0)],
}
TAIL = {
    "pe": [("mixw", 15, 0), ("mixv", 15, 0), ("mixv", 15, 1), ("tacc", 14, 0), ("tacc", 14, 1), ("tacc", 14, 2),
           ("mixw", 15, 1), ("mixw", 15, 2), ("mixv", 15, 2), ("mxh", 10, 0), ("tacc", 15, 0), ("tacc", 15, 1),
           ("tacc", 15, 2)] + [("mxh", i, 0) for i in range(11, 16)],
    "s": [("cw", 14, 2), ("sq", 14, 2), ("sq", 15, 0), ("sq", 15, 1), ("srt", 14, 0), ("sq", 15, 2), ("cw", 15, 2), ("srt", 15, 0)],
    "v": [("cw", 14, 1), ("pr", 13, 2), ("pr", 14, 0), ("pr", 14, 1), ("cw", 15, 0), ("pr", 14, 2), ("pr", 15, 0),
          ("cw", 15, 1), ("pr", 15, 1), ("bia", 9, 0), ("pr", 15, 2), ("qvn", 13, 0), ("bia", 10, 0), ("bia", 11, 0),
          ("qvn", 15, 0)] + [("bia", i, 0) for i in range(12, 16)],
}
SPLICE = {
    "pe": [(("tin", 3, 0), [("w1t", 0, 0)]), (("tin", 4, 0), [("w1t", 1, 0)]), (("tin", 5, 0), [("b1m", 0, 0)])],
    "v": [(("cpo", 3, 0), [("w1c", 0, 0)]), (("cpo", 4, 0), [("w1c", 1, 0)]), (("cpo", 5, 0), [("b1c", 0, 0)]),
          (("pr", 2, 2), [("qw1", 0, 0)])],
}
LATE_LOADS = {1: [("mu", 4), ("q", 4)], 4: [("mu", 5)]}


def tile_painnmixing_pa_t_kernel(tc, q, mu, W_mix, W1, b1, out_0, out_1, out_2):
    nc = tc.nc
    with ExitStack() as ctx:
        const = ctx.enter_context(tc.tile_pool(name="const", bufs=1))
        work = ctx.enter_context(tc.tile_pool(name="work", bufs=2))
        psum = ctx.enter_context(tc.psum_pool(name="psum", bufs=1))
        ctx.enter_context(tc.manual_schedule())

        q_v = q.rearrange("(p t) o k -> p t (o k)", t=NT)
        mu_v = mu.rearrange("(p t) c k -> p t c k", t=NT)
        h_v = out_0.rearrange("(p t) o g -> p t (o g)", t=NT)
        muw_v = out_1.rearrange("(p t) c f -> p t (c f)", t=NT)
        vw_v = out_2.rearrange("(p t) o f -> p t (o f)", t=NT)
        wm_v = [W_mix[0:F, :].rearrange("(p r) k -> p r k", r=4), W_mix[F:2 * F, :].rearrange("(r p) k -> p r k", p=P)]
        wm_half = [[wm_v[j][:, 2 * b:2 * b + 2, :] for b in range(2)] for j in range(2)]
        w1_v = W1.rearrange("(r p) k -> p r k", p=P)

        mu_sb = [const.tile([P, t1 - t0, C, F], BF16, name="mu_sb%d" % j) for j, (t0, t1) in enumerate(MU_CHUNKS)]
        q_sb = [const.tile([P, t1 - t0, F], BF16, name="q_sb%d" % j) for j, (t0, t1) in enumerate(Q_CHUNKS)]
        wm_sb = [[const.tile([P, 2, F], BF16, name="wm_sb%d%d" % (j, b)) for b in range(2)] for j in range(2)]
        w1_sb = const.tile([P, 2, 2 * F], BF16, name="w1_sb")
        b1_row = const.tile([P, G], BF16, name="b1_row")
        ones_b = const.tile([P, P], BF16, name="ones_b")
        zer_b = const.tile([P, F], BF16, name="zer_b")
        b1_f = const.tile([P, G], F32, name="b1_f")
        ident_f = const.tile([P, P], F32, name="ident_f")
        eps_t = const.tile([P, 1], F32, name="eps_t")
        warm = const.tile([P, 1], F32, name="warm")
        wm_g = [const.tile([P, 4, P, 4], BF16, name="wm_g%d" % j, align_bytes=64) for j in range(2)]
        wm_codes = const.tile([P, 2 * F], U32, name="wm_codes", align_bytes=64)
        wm_scales = const.tile([P, 2 * F], U8, name="wm_scales", align_bytes=64)
        w1_g = const.tile([P, 2, 2, P, 4], BF16, name="w1_g", align_bytes=64)
        w1_codes = const.tile([P, 2, G], U32, name="w1_codes", align_bytes=64)
        w1_scales = const.tile([P, 2, G], U8, name="w1_scales", align_bytes=64)
        hpre = const.tile([P, NT, G], F32, name="hpre")

        turn = {}

        def bank(kind, shape, dtype, i=-1):
            group, bufs = BANKS[kind]
            k = turn.get(group, 0)
            turn[group] = k + 1
            return psum.tile(shape, dtype, name=kind + "_ps", tag="%s%d" % (group, k % bufs), bufs=1)

        def mu_rows(i, c):
            for j, (t0, t1) in enumerate(MU_CHUNKS):
                if t0 <= i < t1:
                    return mu_sb[j][:].bitcast(F32)[:, i - t0, c, :]
            return None

        def q_rows(i):
            for j, (t0, t1) in enumerate(Q_CHUNKS):
                if t0 <= i < t1:
                    return q_sb[j][:].bitcast(F32)[:, i - t0, :]
            return None

        def load_mu(j):
            t0, t1 = MU_CHUNKS[j]
            nc.sync.dma_start(out=mu_sb[j][:], in_=mu_v[:, t0:t1, :, :])

        def load_q(j):
            t0, t1 = Q_CHUNKS[j]
            nc.sync.dma_start(out=q_sb[j][:], in_=q_v[:, t0:t1, :])

        nc.vector.memset(zer_b[:].bitcast(U32), 0)
        nc.vector.memset(b1_row[:], 0.0)
        nc.vector.memset(ones_b[:], 1.0)
        for b in range(2):
            nc.sync.dma_start(out=wm_sb[0][b][:], in_=wm_half[0][b])
        load_mu(0)
        load_q(0)
        for b in range(2):
            nc.sync.dma_start(out=wm_sb[1][b][:], in_=wm_half[1][b])
        load_mu(1)
        load_q(1)
        load_mu(2)
        load_q(2)
        nc.sync.dma_start(out=w1_sb[:], in_=w1_v)
        nc.sync.dma_start(out=b1_row[0:1, :], in_=b1.rearrange("(o g) -> o g", o=1))
        load_mu(3)
        load_q(3)

        nc.vector.memset(eps_t[:], EPS)
        make_identity(nc, ident_f[:])
        nc.scalar.activation(out=warm[:], in_=eps_t[:], func=ACT.Sqrt)

        st = {}

        def word_transposes(dst, sources):
            for r, src in enumerate(sources):
                for u in range(2):
                    nc.tensor.transpose(dst[:, r, u, :], src[:, u:2 * P:2], ident_f[:])

        def copy_out(eng, dst, src):
            if eng == "v":
                nc.vector.tensor_copy(out=dst, in_=src)
            else:
                nc.scalar.copy(out=dst, in_=src)

        def op_tin(eng, i, half):
            dst = bank("tin", [P, 2, 2, P], F32)
            if ("g", i) not in st:
                st["g", i] = work.tile([P, 4, P, 4], BF16, name="g", tag="g", bufs=3, align_bytes=64)
            if half == 0:
                word_transposes(dst, [mu_rows(i, 0), mu_rows(i, 1)])
            else:
                word_transposes(dst, [mu_rows(i, 2), q_rows(i)])
            st["tin", i, half] = dst

        def op_cpo(eng, i, half):
            copy_out(eng, st["g", i][:].bitcast(F32)[:, 2 * half:2 * half + 2, :, :],
                     st["tin", i, half][:].rearrange("p r u a -> p r a u"))

        def op_quant(eng, i, a):
            codes = work.tile([P, 4 * P], U32, name="codes", tag="codes", bufs=6, align_bytes=64)
            scales = work.tile([P, 4 * P], U8, name="scales", tag="scales", bufs=6, align_bytes=64)
            nc.vector.quantize_mx(out=codes[:].bitcast(FP8X4), scales=scales[:],
                                  in_=st["g", i][:].rearrange("p r a t -> p (r a t)"))
            st["codes", i] = codes
            st["scales", i] = scales

        def mix_one(i, c, which):
            codes, scales = st["codes", i], st["scales", i]
            dst = bank(which, [P, F], F32, i)
            lo = F if which == "w" else 0
            nc.tensor.matmul_mx(
                out=dst[:],
                lhsT=codes[:, c * P:(c + 1) * P].bitcast(FP8X4),
                lhsT_scale=scales[:, c * P:(c + 1) * P],
                rhs=wm_codes[:, lo:lo + F].bitcast(FP8X4),
                rhs_scale=wm_scales[:, lo:lo + F],
                start=True,
                stop=True,
            )
            st[which, i, c] = dst

        def op_mixw(eng, i, c):
            mix_one(i, c, "w")

        def op_mixv(eng, i, c):
            mix_one(i, c, "v")

        def op_cw(eng, i, c):
            if ("wout", i) not in st:
                st["wout", i] = work.tile([P, C, F], F32, name="wout", tag="wout", bufs=4)
            copy_out(eng, st["wout", i][:, c, :], st["w", i, c][:])

        def op_sq(eng, i, c):
            sq_t = work.tile([P, F], F32, name="sq", tag="sq", bufs=8)
            nc.scalar.activation(out=sq_t[:], in_=st["v", i, c][:], func=ACT.Square)
            st["sq", i, c] = sq_t

        def op_pr(eng, i, c):
            if c == 0:
                st["prod", i] = work.tile([P, C, F], F32, name="prod", tag="prod", bufs=3)
            prod = st["prod", i]
            nc.vector.tensor_tensor(out=prod[:, c, :].rearrange("p (m t) -> p m t", t=4),
                                    in0=st["v", i, c][:].rearrange("p (t m) -> p m t", t=4),
                                    in1=st["wout", i][:, c, :].rearrange("p (m t) -> p m t", t=4), op=ALU.mult)

        def op_add(eng, i, c):
            prod = st["prod", i]
            if c == 1:
                acc = work.tile([P, F], F32, name="acc", tag="acc", bufs=2)
                nc.gpsimd.tensor_tensor(out=acc[:], in0=prod[:, 0, :], in1=prod[:, 1, :], op=ALU.add)
                st["acc", i] = acc
            else:
                vw = work.tile([P, F], F32, name="vw", tag="vw", bufs=4)
                nc.gpsimd.tensor_tensor(out=vw[:], in0=st["acc", i][:], in1=prod[:, 2, :], op=ALU.add)
                st["vw", i] = vw

        def op_tacc(eng, i, c):
            if c == 0:
                st["ss", i] = bank("ss", [P, 4, P], F32, i)
            ss = st["ss", i]
            for t in range(4):
                nc.tensor.matmul(out=ss[:, t, :], lhsT=st["sq", i, c][:, t * P:(t + 1) * P], rhs=ident_f[:],
                                 is_transpose=True, start=(c == 0 and t == 0), stop=(c == C - 1 and t == 3))

        def op_srt(eng, i, a):
            if i % 2 == 0:
                st["vn_g", i // 2] = work.tile([P, 2, P, 4], BF16, name="vn_g", tag="vn_g", bufs=3, align_bytes=64)
            nc.scalar.activation(out=st["vn_g", i // 2][:, i % 2, :, :], in_=st["ss", i][:].rearrange("p t a -> p a t"), func=ACT.Sqrt,
                                 bias=EPS, scale=1.0)

        def op_qvn(eng, i, a):
            vn_codes = work.tile([P, 2 * P], U32, name="vn_codes", tag="vn_codes", bufs=NT // 2, align_bytes=64)
            vn_scales = work.tile([P, 2 * P], U8, name="vn_scales", tag="vn_scales", bufs=NT // 2, align_bytes=64)
            nc.vector.quantize_mx(out=vn_codes[:].bitcast(FP8X4), scales=vn_scales[:],
                                  in_=st["vn_g", i // 2][:].rearrange("p j a t -> p (j a t)"))
            for j in range(2):
                st["vn_codes", i - 1 + j] = vn_codes[:, j * P:(j + 1) * P]
                st["vn_scales", i - 1 + j] = vn_scales[:, j * P:(j + 1) * P]

        def op_mxh(eng, i, a):
            h_ps = bank("h", [P, G], F32, i)
            nc.tensor.matmul_mx(out=h_ps[:], lhsT=st["codes", i][:, 3 * P:4 * P].bitcast(FP8X4),
                                lhsT_scale=st["scales", i][:, 3 * P:4 * P], rhs=w1_codes[:, 0, :].bitcast(FP8X4),
                                rhs_scale=w1_scales[:, 0, :], start=True, stop=False)
            nc.tensor.matmul_mx(out=h_ps[:], lhsT=st["vn_codes", i].bitcast(FP8X4), lhsT_scale=st["vn_scales", i],
                                rhs=w1_codes[:, 1, :].bitcast(FP8X4), rhs_scale=w1_scales[:, 1, :], start=False, stop=True)
            st["h_ps", i] = h_ps

        def op_bia(eng, i, a):
            nc.vector.tensor_tensor(out=hpre[:, i, :], in0=st["h_ps", i][:], in1=b1_f[:], op=ALU.add)

        def op_wmt(eng, j, b):
            wf = wm_sb[j][b][:].bitcast(F32)
            dst = bank("wm", [P, 2, 2, P], F32)
            word_transposes(dst, [wf[:, 0, :], wf[:, 1, :]])
            st["wm_ps", j, b] = dst

        def op_wmc(eng, j, b):
            copy_out(eng, wm_g[j][:].bitcast(F32)[:, 2 * b:2 * b + 2, :, :],
                     st["wm_ps", j, b][:].rearrange("p r u a -> p r a u"))

        def op_qwm(eng, j, a):
            nc.vector.quantize_mx(out=wm_codes[:, j * F:(j + 1) * F].bitcast(FP8X4),
                                  scales=wm_scales[:, j * F:(j + 1) * F],
                                  in_=wm_g[j][:].rearrange("p r a t -> p (r a t)"))

        def op_w1t(eng, j, a):
            wf = w1_sb[:].bitcast(F32)
            dst = bank("w1", [P, 2, 2, P], F32)
            word_transposes(dst, [wf[:, 0, j * 2 * P:(j + 1) * 2 * P], wf[:, 1, j * 2 * P:(j + 1) * 2 * P]])
            st["w1_ps", j] = dst

        def op_w1c(eng, j, a):
            copy_out(eng, w1_g[:].bitcast(F32)[:, j, :, :, :], st["w1_ps", j][:].rearrange("p r u a -> p r a u"))

        def op_b1m(eng, j, a):
            dst = bank("w1", [P, G], F32)
            nc.tensor.matmul(out=dst[:], lhsT=ones_b[:], rhs=b1_row[:], start=True, stop=True)
            st["b1_ps"] = dst

        def op_dmy(eng, j, a):
            dst = bank("dmy", [P, F], F32)
            nc.tensor.matmul(out=dst[:], lhsT=zer_b[:, 0:P], rhs=zer_b[:], start=True, stop=True)

        def op_b1c(eng, j, a):
            nc.vector.tensor_copy(out=b1_f[:], in_=st["b1_ps"][:])

        def op_qw1(eng, j, a):
            nc.vector.quantize_mx(out=w1_codes[:].rearrange("p j g -> p (j g)").bitcast(FP8X4),
                                  scales=w1_scales[:].rearrange("p j g -> p (j g)"),
                                  in_=w1_g[:].rearrange("p j r a t -> p (j r a t)"))

        def op_stw(eng, i, a):
            nc.sync.dma_start(out=muw_v[:, i, :], in_=st["wout", i][:].rearrange("p c f -> p (c f)"))
            for kind, j in LATE_LOADS.get(i, []):
                if kind == "mu":
                    load_mu(j)
                else:
                    load_q(j)

        def op_stvw(eng, i, a):
            nc.sync.dma_start(out=vw_v[:, i, :], in_=st["vw", i][:])

        def op_silu(eng, t0, t1):
            nc.scalar.activation(out=hpre[:, t0:t1, :], in_=hpre[:, t0:t1, :], func=ACT.Silu)

        def op_sth(eng, t0, t1):
            nc.sync.dma_start(out=h_v[:, t0:t1, :], in_=hpre[:, t0:t1, :])

        OPS = {"tin": op_tin, "cpo": op_cpo, "quant": op_quant, "mixw": op_mixw, "mixv": op_mixv, "cw": op_cw,
               "sq": op_sq, "pr": op_pr, "add": op_add, "tacc": op_tacc, "srt": op_srt, "qvn": op_qvn, "mxh": op_mxh,
               "bia": op_bia, "wmt": op_wmt, "wmc": op_wmc, "qwm": op_qwm, "w1t": op_w1t, "w1c": op_w1c, "qw1": op_qw1, "b1m": op_b1m, "b1c": op_b1c, "dmy": op_dmy,
               "stw": op_stw, "stvw": op_stvw, "silu": op_silu, "sth": op_sth}

        def needs(op):
            n, i, a = op
            if n == "cpo":
                return [("tin", i, a)]
            if n == "quant":
                return [("cpo", i, 0), ("cpo", i, 1)]
            if n == "mixw":
                return [("quant", i, 0), ("qwm", 1, 0)]
            if n == "mixv":
                return [("quant", i, 0), ("qwm", 0, 0)]
            if n == "cw":
                return [("mixw", i, a)]
            if n == "sq":
                return [("mixv", i, a)]
            if n == "pr":
                return [("cw", i, a), ("mixv", i, a), ("sq", i, a)]
            if n == "add":
                return [("pr", i, 0), ("pr", i, 1)] if a == 1 else [("add", i, 1), ("pr", i, 2)]
            if n == "tacc":
                return [("sq", i, a)] + ([("tacc", i, a - 1)] if a > 0 else [])
            if n == "srt":
                return [("tacc", i, 2)]
            if n == "qvn":
                return [("srt", i - 1, 0), ("srt", i, 0)]
            if n == "mxh":
                return [("qvn", i | 1, 0), ("qw1", 0, 0)]
            if n == "bia":
                return [("mxh", i, 0), ("b1c", 0, 0)]
            if n == "b1c":
                return [("b1m", 0, 0)]
            if n == "wmc":
                return [("wmt", i, a)]
            if n == "qwm":
                return [("wmc", i, 0), ("wmc", i, 1)]
            if n == "w1c":
                return [("w1t", i, 0)]
            if n == "qw1":
                return [("w1c", 0, 0), ("w1c", 1, 0)]
            if n == "stw":
                return [("cw", i, 0), ("cw", i, 1), ("cw", i, 2)]
            if n == "stvw":
                return [("add", i, 2)]
            if n == "silu":
                return [("bia", t, 0) for t in range(i, a)] + [("srt", NT - 1, 0)]
            if n == "sth":
                return [("silu", i, a)]
            return []

        def users(op):
            n, i, a = op
            if n == "tin":
                return [("cpo", i, a)]
            if n == "mixw":
                return [("cw", i, a)]
            if n == "mixv":
                return [("pr", i, a), ("sq", i, a)]
            if n == "tacc":
                return [("srt", i, 0)]
            if n == "mxh":
                return [("bia", i, 0)]
            if n == "wmt":
                return [("wmc", i, a)]
            if n == "w1t":
                return [("w1c", i, 0)]
            if n == "b1m":
                return [("b1c", 0, 0)]
            return []

        KIND = {"b1m": "w1", "dmy": "dmy", "tin": "tin", "mixw": "w", "mixv": "v", "tacc": "ss", "mxh": "h", "wmt": "wm", "w1t": "w1"}

        lists = {}
        for eng in ("pe", "s", "v", "g", "sp"):
            seq = list(HEAD.get(eng, []))
            done = set(seq) | {op for e in HEAD for op in HEAD[e] if op[0] == "cpo"} | set(TAIL.get(eng, []))
            for it in range(-3, NT + 4):
                for n, off, a in STEPS[eng]:
                    op = (n, it + off, a)
                    if not 0 <= it + off < NT or op in done or (n == "qvn" and op[1] % 2 == 0):
                        continue
                    if n == "cw" and ((op[1], a) in V_CW) != (eng == "v"):
                        continue
                    seq.append(op)
                    done.add(op)
            seq.extend(TAIL.get(eng, []))
            for before, extra in SPLICE.get(eng, []):
                k = seq.index(before)
                seq[k:k] = extra
            lists[eng] = seq
        for t0, t1 in SILU_CHUNKS:
            lists["s"].append(("silu", t0, t1))
            lists["sp"].append(("sth", t0, t1))

        emitted = set()
        pos = {eng: 0 for eng in lists}
        alloc = {}
        progress = True
        while progress:
            progress = False
            for eng in ("pe", "s", "v", "g", "sp"):
                while pos[eng] < len(lists[eng]):
                    op = lists[eng][pos[eng]]
                    if not all(x in emitted for x in needs(op)):
                        break
                    if op[0] in KIND and not (op[0] == "tacc" and op[2] > 0):
                        tag, bufs = BANKS[KIND[op[0]]]
                        hist = alloc.get(tag, [])
                        if len(hist) >= bufs and not all(x in emitted for x in users(hist[-bufs])):
                            break
                        alloc[tag] = hist + [op]
                    OPS[op[0]](eng, op[1], op[2])
                    emitted.add(op)
                    pos[eng] += 1
                    progress = True
        assert all(pos[eng] == len(lists[eng]) for eng in lists), "the orders cannot run"
